import numpy as np
import ml_dtypes


def mxq(x, axis, fmt="e4m3"):
    dtype, down = {"e4m3": (ml_dtypes.float8_e4m3fn, 7), "e5m2": (ml_dtypes.float8_e5m2, 14)}[fmt]
    v = np.moveaxis(np.asarray(x, np.float32).astype(ml_dtypes.bfloat16).astype(np.float64), axis, -1)
    blocks = v.reshape(v.shape[:-1] + (-1, 32))
    amax = np.abs(blocks).max(-1, keepdims=True)
    byte = np.maximum(np.where(amax > 0, np.frexp(amax)[1] - 1 + 127, 0) - down, 1)
    scale = np.exp2(byte - 127.0)
    codes = (blocks / scale).astype(np.float32).astype(dtype).astype(np.float64)
    return np.moveaxis((codes * scale).reshape(v.shape), -1, axis)


WIDE = False


def mx_kscale(k):
    if not WIDE:
        return np.ones(k)
    levels = np.array([10, -10, 5, -5, 0])
    a = np.random.permutation(np.resize(levels, k // 512 * 4)).reshape(k // 512, 4)
    idx = np.arange(k)
    return np.exp2(a[idx // 512, idx % 128 // 32])


BF16 = ml_dtypes.bfloat16


def bf(x):
    return np.asarray(x, np.float32).astype(BF16)


def f64(x):
    return np.asarray(x).astype(np.float64)


S, E, H, DH = 1024, 1024, 16, 64
W = H * DH


def rotate_half(t):
    return np.stack((-t[..., 1::2], t[..., ::2]), axis=-1).reshape(t.shape)


def setup_inputs():
    s = mx_kscale(E)
    return {"hidden_states": bf(np.random.standard_normal((S, E)) * s),
            "cos": bf(np.random.uniform(size=(S, DH))),
            "sin": bf(np.random.uniform(size=(S, DH))),
            "w_qkv": bf(np.random.standard_normal((E, 3 * W)) * 2.0 / np.sqrt(E) / s[:, None]),
            "b_qkv": bf(np.random.standard_normal(3 * W) * 0.3)}


def reference(hidden_states, cos, sin, w_qkv, b_qkv):
    qkv = ((mxq(f64(hidden_states), 1, "e4m3") @ mxq(f64(w_qkv), 0, "e4m3")) + f64(b_qkv)).reshape(S, 3, H, DH)
    q, k, v = qkv[:, 0], qkv[:, 1], qkv[:, 2]
    c = f64(cos)[:, None, :]
    sn = f64(sin)[:, None, :]
    q_rot = q * c + rotate_half(q) * sn
    k_rot = k * c + rotate_half(k) * sn
    return q_rot, k_rot, v

@@ -1,0 +1,297 @@
+from contextlib import ExitStack
+
+import concourse.mybir as mybir
+from concourse.masks import make_identity
+
+F32 = mybir.dt.float32
+BF16 = mybir.dt.bfloat16
+U32 = mybir.dt.uint32
+U8 = mybir.dt.uint8
+FP8X4 = mybir.dt.float8_e4m3fn_x4
+ADD = mybir.AluOpType.add
+MULT = mybir.AluOpType.mult
+IDENTITY = mybir.ActivationFunctionType.Identity
+
+S, E, HEADS, DH = 1024, 1024, 16, 64
+WIDTH = HEADS * DH
+HALF = DH // 2
+P = 128
+PACK = 4
+K_PASS = P * PACK
+PASSES = E // K_PASS
+S_BLOCKS = S // P
+CHUNK_BLOCKS = 4
+CHUNK = CHUNK_BLOCKS * P
+CHUNKS = S_BLOCKS // CHUNK_BLOCKS
+GROUP = 512
+GROUPS = 3 * WIDTH // GROUP
+ROTATED_GROUPS = 2 * WIDTH // GROUP
+GROUP_TILES = GROUP // P
+GROUP_HEADS = GROUP // DH
+PAIR = 2
+
+FLOPS = 2 * S * E * 3 * WIDTH
+
+
+def tile_arlowvisionattention_pa_kernel(
+    tc, hidden_states, cos, sin, w_qkv, b_qkv, out_0, out_1, out_2
+):
+    nc = tc.nc
+    with ExitStack() as ctx:
+        const = ctx.enter_context(tc.tile_pool(name="const", bufs=1))
+        operands = ctx.enter_context(tc.tile_pool(name="operands", bufs=1))
+        work = ctx.enter_context(tc.tile_pool(name="work", bufs=3))
+        psum_mx = ctx.enter_context(tc.psum_pool(name="psum_mx", bufs=4))
+        psum_plain = ctx.enter_context(tc.psum_pool(name="psum_plain", bufs=4))
+
+        x_rows = hidden_states.rearrange("(p b) k -> p b k", b=S_BLOCKS)
+        out_rows = [
+            out.rearrange("(p b) h d -> p b (h d)", b=S_BLOCKS) for out in (out_0, out_1, out_2)
+        ]
+
+        x_raw = [
+            operands.tile([P, CHUNK_BLOCKS, E], BF16, name="x_raw%d" % c) for c in range(CHUNKS)
+        ]
+        x_grouped = [
+            operands.tile([P, PASSES, CHUNK, PACK], BF16, name="x_grouped%d" % c, align_bytes=64)
+            for c in range(CHUNKS)
+        ]
+        x_codes = [
+            operands.tile([P, PASSES, CHUNK], U32, name="x_codes%d" % c, align_bytes=64)
+            for c in range(CHUNKS)
+        ]
+        x_scales = [
+            operands.tile([P, PASSES, CHUNK], U8, name="x_scales%d" % c, align_bytes=64)
+            for c in range(CHUNKS)
+        ]
+        w_raw = [
+            operands.tile([P, PASSES, PACK, GROUP], BF16, name="w_raw%d" % n) for n in range(GROUPS)
+        ]
+        w_codes = [
+            operands.tile([P, PASSES, GROUP], U32, name="w_codes%d" % n, align_bytes=64)
+            for n in range(GROUPS)
+        ]
+        w_scales = [
+            operands.tile([P, PASSES, GROUP], U8, name="w_scales%d" % n, align_bytes=64)
+            for n in range(GROUPS)
+        ]
+
+        cos_raw = const.tile([P, S_BLOCKS, DH], BF16)
+        sin_raw = const.tile([P, S_BLOCKS, DH], BF16)
+        nc.scalar.dma_start(out=cos_raw[:], in_=cos.rearrange("(p b) d -> p b d", b=S_BLOCKS))
+        nc.scalar.dma_start(out=sin_raw[:], in_=sin.rearrange("(p b) d -> p b d", b=S_BLOCKS))
+
+        rotated_tiles = ROTATED_GROUPS * GROUP_TILES
+        bias_rows = const.tile([P, P], BF16)
+        nc.vector.memset(bias_rows[:], 0.0)
+        nc.scalar.dma_start(
+            out=bias_rows[0:rotated_tiles, :],
+            in_=b_qkv[0 : rotated_tiles * P].rearrange("(t n) -> t n", n=P),
+        )
+        v_bias_row = const.tile([P, WIDTH], BF16)
+        nc.vector.memset(v_bias_row[:], 0.0)
+        nc.scalar.dma_start(
+            out=v_bias_row[0:1, :],
+            in_=b_qkv[2 * WIDTH : 3 * WIDTH].rearrange("(o n) -> o n", o=1),
+        )
+
+        def load_weights(n):
+            for g in range(PASSES):
+                for u in range(PACK // 2):
+                    first = g * K_PASS + u * 2 * P
+                    nc.sync.dma_start(
+                        out=w_raw[n][:, g, 2 * u : 2 * u + 2, :],
+                        in_=w_qkv[first : first + 2 * P, n * GROUP : (n + 1) * GROUP].rearrange(
+                            "(q e) n -> q e n", e=2
+                        ),
+                    )
+
+        load_weights(0)
+        for c in range(CHUNKS):
+            nc.sync.dma_start(
+                out=x_raw[c][:], in_=x_rows[:, c * CHUNK_BLOCKS : (c + 1) * CHUNK_BLOCKS, :]
+            )
+        for n in range(1, GROUPS):
+            load_weights(n)
+
+        ident = const.tile([P, P], F32)
+        make_identity(nc, ident[:])
+        evens_first = const.tile([P, P], F32)
+        nc.vector.tensor_copy(
+            out=evens_first[:].rearrange("r (h two i) -> r h two i", two=2, i=HALF),
+            in_=ident[:].rearrange("r (h i two) -> r h two i", two=2, i=HALF),
+        )
+
+        cos_split = const.tile([P, S_BLOCKS, 2, HALF], F32)
+        sin_split = const.tile([P, S_BLOCKS, 2, HALF], F32)
+        sin_sorted = sin_raw[:].rearrange("p b (i two) -> p b two i", two=2)
+        nc.vector.tensor_copy(
+            out=cos_split[:], in_=cos_raw[:].rearrange("p b (i two) -> p b two i", two=2)
+        )
+        nc.vector.tensor_scalar_mul(
+            out=sin_split[:, :, 0, :], in0=sin_sorted[:, :, 0, :], scalar1=-1.0
+        )
+        nc.vector.tensor_copy(out=sin_split[:, :, 1, :], in_=sin_sorted[:, :, 1, :])
+
+        def quantise_weights(n, g):
+            grouped = work.tile([P, GROUP, PACK], BF16, align_bytes=64, tag="w_grouped")
+            nc.scalar.copy(
+                out=grouped[:].rearrange("q (c i) t -> q c t i", i=4),
+                in_=w_raw[n][:, g, :, :].rearrange("q t (c i) -> q c t i", i=4),
+            )
+            nc.vector.quantize_mx(
+                out=w_codes[n][:, g, :].bitcast(FP8X4),
+                scales=w_scales[n][:, g, :],
+                in_=grouped[:].rearrange("q c t -> q (c t)"),
+            )
+
+        def quantise_positions(c):
+            grouped_words = x_grouped[c][:].bitcast(F32)
+            for j in range(CHUNK_BLOCKS):
+                words = x_raw[c][:, j, :].bitcast(F32)
+                flipped = psum_plain.tile([P, PASSES * 2, P], F32, tag="plain")
+                for gu in range(PASSES * 2):
+                    nc.tensor.transpose(
+                        out=flipped[:, gu, :], in_=words[:, gu * P : (gu + 1) * P], identity=ident[:]
+                    )
+                nc.vector.tensor_copy(
+                    out=grouped_words[:, :, j * P : (j + 1) * P, :],
+                    in_=flipped[:].rearrange("q (g u) s -> q g s u", u=2),
+                )
+            for g in range(PASSES):
+                nc.vector.quantize_mx(
+                    out=x_codes[c][:, g, :].bitcast(FP8X4),
+                    scales=x_scales[c][:, g, :],
+                    in_=x_grouped[c][:, g, :, :].rearrange("q s t -> q (s t)"),
+                )
+
+        for g in range(PASSES):
+            quantise_weights(0, g)
+        for c in range(CHUNKS):
+            quantise_positions(c)
+
+        bias_rows_f32 = const.tile([P, P], F32)
+        nc.vector.tensor_copy(out=bias_rows_f32[:], in_=bias_rows[:])
+        bias_flipped = psum_plain.tile([P, P], F32, tag="plain")
+        nc.tensor.transpose(out=bias_flipped[:], in_=bias_rows_f32[:], identity=ident[:])
+        bias_cols = const.tile([P, rotated_tiles], F32)
+        nc.vector.tensor_copy(out=bias_cols[:], in_=bias_flipped[:, 0:rotated_tiles])
+        ones = const.tile([P, P], BF16)
+        nc.vector.memset(ones[:], 1.0)
+        v_bias = const.tile([P, WIDTH], F32)
+        for n in range(WIDTH // GROUP):
+            spread = psum_plain.tile([P, GROUP], F32, tag="plain")
+            nc.tensor.matmul(
+                out=spread[:],
+                lhsT=ones[:],
+                rhs=v_bias_row[:, n * GROUP : (n + 1) * GROUP],
+                start=True,
+                stop=True,
+            )
+            nc.vector.tensor_copy(out=v_bias[:, n * GROUP : (n + 1) * GROUP], in_=spread[:])
+
+        def project_rotated(n, c):
+            biased = []
+            for m in range(GROUP_TILES):
+                acc = psum_mx.tile([P, CHUNK], F32, tag="acc")
+                for g in range(PASSES):
+                    nc.tensor.matmul_mx(
+                        out=acc[:],
+                        lhsT=w_codes[n][:, g, m * P : (m + 1) * P].bitcast(FP8X4),
+                        lhsT_scale=w_scales[n][:, g, m * P : (m + 1) * P],
+                        rhs=x_codes[c][:, g, :].bitcast(FP8X4),
+                        rhs_scale=x_scales[c][:, g, :],
+                        start=(g == 0),
+                        stop=(g == PASSES - 1),
+                    )
+                with_bias = work.tile([P, CHUNK], F32, tag="with_bias", bufs=2 * GROUP_TILES)
+                tile_index = n * GROUP_TILES + m
+                nc.scalar.activation(
+                    out=with_bias[:],
+                    in_=acc[:],
+                    func=IDENTITY,
+                    bias=bias_cols[:, tile_index : tile_index + 1],
+                    scale=1.0,
+                )
+                biased.append(with_bias)
+
+            for first in range(0, CHUNK_BLOCKS, PAIR):
+                by_cos = work.tile([P, PAIR, GROUP], F32, tag="by_cos")
+                by_sin = work.tile([P, PAIR, GROUP], F32, tag="by_sin")
+                for jj in range(PAIR):
+                    j = first + jj
+                    b = c * CHUNK_BLOCKS + j
+                    y = psum_plain.tile([P, GROUP], F32, tag="plain")
+                    for m in range(GROUP_TILES):
+                        nc.tensor.transpose(
+                            out=y[:, m * P : (m + 1) * P],
+                            in_=biased[m][:, j * P : (j + 1) * P],
+                            identity=evens_first[:],
+                        )
+                    nc.vector.tensor_tensor(
+                        out=by_cos[:, jj, :].rearrange("p (h x) -> p h x", x=DH),
+                        in0=y[:].rearrange("p (h x) -> p h x", x=DH),
+                        in1=cos_split[:, b, :, :]
+                        .rearrange("p two i -> p (two i)")
+                        .unsqueeze(1)
+                        .to_broadcast([P, GROUP_HEADS, DH]),
+                        op=MULT,
+                    )
+                    y_halves = y[:].rearrange("p (h two i) -> p h two i", two=2, i=HALF)
+                    sin_halves = by_sin[:, jj, :].rearrange("p (h two i) -> p h two i", two=2, i=HALF)
+                    for two in range(2):
+                        nc.vector.tensor_tensor(
+                            out=sin_halves[:, :, two, :],
+                            in0=y_halves[:, :, 1 - two, :],
+                            in1=sin_split[:, b, two, :]
+                            .unsqueeze(1)
+                            .to_broadcast([P, GROUP_HEADS, HALF]),
+                            op=MULT,
+                        )
+                rotated = work.tile([P, PAIR, GROUP], F32, tag="result")
+                nc.gpsimd.tensor_tensor(
+                    out=rotated[:].rearrange("p j (h i two) -> p (j h) i two", i=HALF, two=2),
+                    in0=by_cos[:].rearrange("p j (h two i) -> p (j h) i two", i=HALF, two=2),
+                    in1=by_sin[:].rearrange("p j (h two i) -> p (j h) i two", i=HALF, two=2),
+                    op=ADD,
+                )
+                store(n, c * CHUNK_BLOCKS + first, rotated)
+
+        def project_plain(n, c):
+            for first in range(0, CHUNK_BLOCKS, PAIR):
+                plain = work.tile([P, PAIR, GROUP], F32, tag="result")
+                for jj in range(PAIR):
+                    j = first + jj
+                    acc = psum_mx.tile([P, GROUP], F32, tag="acc")
+                    for g in range(PASSES):
+                        nc.tensor.matmul_mx(
+                            out=acc[:],
+                            lhsT=x_codes[c][:, g, j * P : (j + 1) * P].bitcast(FP8X4),
+                            lhsT_scale=x_scales[c][:, g, j * P : (j + 1) * P],
+                            rhs=w_codes[n][:, g, :].bitcast(FP8X4),
+                            rhs_scale=w_scales[n][:, g, :],
+                            start=(g == 0),
+                            stop=(g == PASSES - 1),
+                        )
+                    col = (n - ROTATED_GROUPS) * GROUP
+                    nc.vector.tensor_tensor(
+                        out=plain[:, jj, :], in0=acc[:], in1=v_bias[:, col : col + GROUP], op=ADD
+                    )
+                store(n, c * CHUNK_BLOCKS + first, plain)
+
+        def store(n, first_block, result):
+            which, col = divmod(n * GROUP, WIDTH)
+            nc.sync.dma_start(
+                out=out_rows[which][:, first_block : first_block + PAIR, col : col + GROUP],
+                in_=result[:],
+            )
+
+        assert PASSES == CHUNKS
+        for n in range(GROUPS):
+            for c in range(CHUNKS):
+                if n + 1 < GROUPS:
+                    quantise_weights(n + 1, c)
+                if n < ROTATED_GROUPS:
+                    project_rotated(n, c)
+                else:
+                    project_plain(n, c)

@@ -10,7 +10,6 @@ U8 = mybir.dt.uint8
 FP8X4 = mybir.dt.float8_e4m3fn_x4
 ADD = mybir.AluOpType.add
 MULT = mybir.AluOpType.mult
-IDENTITY = mybir.ActivationFunctionType.Identity
 
 S, E, HEADS, DH = 1024, 1024, 16, 64
 WIDTH = HEADS * DH
@@ -27,7 +26,7 @@ GROUP = 512
 GROUPS = 3 * WIDTH // GROUP
 ROTATED_GROUPS = 2 * WIDTH // GROUP
 GROUP_TILES = GROUP // P
-GROUP_HEADS = GROUP // DH
+TILE_HEADS = P // DH
 PAIR = 2
 
 FLOPS = 2 * S * E * 3 * WIDTH
@@ -41,8 +40,8 @@ def tile_arlowvisionattention_pa_kernel(
         const = ctx.enter_context(tc.tile_pool(name="const", bufs=1))
         operands = ctx.enter_context(tc.tile_pool(name="operands", bufs=1))
         work = ctx.enter_context(tc.tile_pool(name="work", bufs=3))
-        psum_mx = ctx.enter_context(tc.psum_pool(name="psum_mx", bufs=4))
-        psum_plain = ctx.enter_context(tc.psum_pool(name="psum_plain", bufs=4))
+        psum_mx = ctx.enter_context(tc.psum_pool(name="psum_mx", bufs=5))
+        psum_plain = ctx.enter_context(tc.psum_pool(name="psum_plain", bufs=3))
 
         x_rows = hidden_states.rearrange("(p b) k -> p b k", b=S_BLOCKS)
         out_rows = [
@@ -116,22 +115,55 @@ def tile_arlowvisionattention_pa_kernel(
 
         ident = const.tile([P, P], F32)
         make_identity(nc, ident[:])
-        evens_first = const.tile([P, P], F32)
+        swap = const.tile([P, P], F32)
+        swap_pairs = swap[:].rearrange("r (i two) -> r i two", two=2)
+        ident_pairs = ident[:].rearrange("r (i two) -> r i two", two=2)
+        for two in range(2):
+            nc.vector.tensor_copy(out=swap_pairs[:, :, two], in_=ident_pairs[:, :, 1 - two])
+
+        bias_rows_f32 = const.tile([P, P], F32)
+        nc.vector.tensor_copy(out=bias_rows_f32[:], in_=bias_rows[:])
+        bias_flipped = psum_plain.tile([P, P], F32, tag="plain")
+        nc.tensor.transpose(out=bias_flipped[:], in_=bias_rows_f32[:], identity=ident[:])
+        bias_cols = const.tile([P, rotated_tiles], F32)
+        nc.vector.tensor_copy(out=bias_cols[:], in_=bias_flipped[:, 0:rotated_tiles])
+
+        own_factor = const.tile([P, S_BLOCKS, TILE_HEADS, DH], F32)
         nc.vector.tensor_copy(
-            out=evens_first[:].rearrange("r (h two i) -> r h two i", two=2, i=HALF),
-            in_=ident[:].rearrange("r (h i two) -> r h two i", two=2, i=HALF),
+            out=own_factor[:],
+            in_=cos_raw[:].unsqueeze(2).to_broadcast([P, S_BLOCKS, TILE_HEADS, DH]),
+        )
+        sin_pairs = sin_raw[:].rearrange("p b (i two) -> p b i two", two=2)
+        crossed = const.tile([P, S_BLOCKS, HALF, 2], F32)
+        nc.vector.tensor_copy(out=crossed[:, :, :, 0], in_=sin_pairs[:, :, :, 1])
+        nc.vector.tensor_scalar_mul(out=crossed[:, :, :, 1], in0=sin_pairs[:, :, :, 0], scalar1=-1.0)
+        neighbour_factor = const.tile([P, S_BLOCKS, TILE_HEADS, DH], F32)
+        nc.vector.tensor_copy(
+            out=neighbour_factor[:],
+            in_=crossed[:]
+            .rearrange("p b i two -> p b (i two)")
+            .unsqueeze(2)
+            .to_broadcast([P, S_BLOCKS, TILE_HEADS, DH]),
         )
 
-        cos_split = const.tile([P, S_BLOCKS, 2, HALF], F32)
-        sin_split = const.tile([P, S_BLOCKS, 2, HALF], F32)
-        sin_sorted = sin_raw[:].rearrange("p b (i two) -> p b two i", two=2)
-        nc.vector.tensor_copy(
-            out=cos_split[:], in_=cos_raw[:].rearrange("p b (i two) -> p b two i", two=2)
-        )
-        nc.vector.tensor_scalar_mul(
-            out=sin_split[:, :, 0, :], in0=sin_sorted[:, :, 0, :], scalar1=-1.0
-        )
-        nc.vector.tensor_copy(out=sin_split[:, :, 1, :], in_=sin_sorted[:, :, 1, :])
+        def flip_table(table, c):
+            flipped = psum_plain.tile([P, CHUNK_BLOCKS, P], F32, tag="plain")
+            for j in range(CHUNK_BLOCKS):
+                nc.tensor.transpose(
+                    out=flipped[:, j, :],
+                    in_=table[:, c * CHUNK_BLOCKS + j, :, :].rearrange("p h d -> p (h d)"),
+                    identity=ident[:],
+                )
+            return flipped
+
+        cos_t = const.tile([P, CHUNKS, CHUNK], F32)
+        sin_t = const.tile([P, CHUNKS, CHUNK], F32)
+        for c in range(CHUNKS):
+            for table, table_t in ((own_factor, cos_t), (neighbour_factor, sin_t)):
+                nc.scalar.copy(
+                    out=table_t[:, c, :],
+                    in_=flip_table(table, c)[:].rearrange("r j p -> r (j p)"),
+                )
 
         def quantise_weights(n, g):
             grouped = work.tile([P, GROUP, PACK], BF16, align_bytes=64, tag="w_grouped")
@@ -165,33 +197,8 @@ def tile_arlowvisionattention_pa_kernel(
                     in_=x_grouped[c][:, g, :, :].rearrange("q s t -> q (s t)"),
                 )
 
-        for g in range(PASSES):
-            quantise_weights(0, g)
-        for c in range(CHUNKS):
-            quantise_positions(c)
-
-        bias_rows_f32 = const.tile([P, P], F32)
-        nc.vector.tensor_copy(out=bias_rows_f32[:], in_=bias_rows[:])
-        bias_flipped = psum_plain.tile([P, P], F32, tag="plain")
-        nc.tensor.transpose(out=bias_flipped[:], in_=bias_rows_f32[:], identity=ident[:])
-        bias_cols = const.tile([P, rotated_tiles], F32)
-        nc.vector.tensor_copy(out=bias_cols[:], in_=bias_flipped[:, 0:rotated_tiles])
-        ones = const.tile([P, P], BF16)
-        nc.vector.memset(ones[:], 1.0)
-        v_bias = const.tile([P, WIDTH], F32)
-        for n in range(WIDTH // GROUP):
-            spread = psum_plain.tile([P, GROUP], F32, tag="plain")
-            nc.tensor.matmul(
-                out=spread[:],
-                lhsT=ones[:],
-                rhs=v_bias_row[:, n * GROUP : (n + 1) * GROUP],
-                start=True,
-                stop=True,
-            )
-            nc.vector.tensor_copy(out=v_bias[:, n * GROUP : (n + 1) * GROUP], in_=spread[:])
-
-        def project_rotated(n, c):
-            biased = []
+        def multiply_rotated(n, c):
+            products = []
             for m in range(GROUP_TILES):
                 acc = psum_mx.tile([P, CHUNK], F32, tag="acc")
                 for g in range(PASSES):
@@ -204,70 +211,59 @@ def tile_arlowvisionattention_pa_kernel(
                         start=(g == 0),
                         stop=(g == PASSES - 1),
                     )
-                with_bias = work.tile([P, CHUNK], F32, tag="with_bias", bufs=2 * GROUP_TILES)
                 tile_index = n * GROUP_TILES + m
-                nc.scalar.activation(
-                    out=with_bias[:],
-                    in_=acc[:],
-                    func=IDENTITY,
-                    bias=bias_cols[:, tile_index : tile_index + 1],
-                    scale=1.0,
-                )
-                biased.append(with_bias)
-
-            for first in range(0, CHUNK_BLOCKS, PAIR):
-                by_cos = work.tile([P, PAIR, GROUP], F32, tag="by_cos")
-                by_sin = work.tile([P, PAIR, GROUP], F32, tag="by_sin")
-                for jj in range(PAIR):
-                    j = first + jj
-                    b = c * CHUNK_BLOCKS + j
-                    y = psum_plain.tile([P, GROUP], F32, tag="plain")
-                    for m in range(GROUP_TILES):
-                        nc.tensor.transpose(
-                            out=y[:, m * P : (m + 1) * P],
-                            in_=biased[m][:, j * P : (j + 1) * P],
-                            identity=evens_first[:],
-                        )
-                    nc.vector.tensor_tensor(
-                        out=by_cos[:, jj, :].rearrange("p (h x) -> p h x", x=DH),
-                        in0=y[:].rearrange("p (h x) -> p h x", x=DH),
-                        in1=cos_split[:, b, :, :]
-                        .rearrange("p two i -> p (two i)")
-                        .unsqueeze(1)
-                        .to_broadcast([P, GROUP_HEADS, DH]),
-                        op=MULT,
+                by_cos = work.tile([P, CHUNK], F32, tag="by_cos", bufs=2 * GROUP_TILES)
+                by_sin = work.tile([P, CHUNK], F32, tag="by_sin", bufs=2 * GROUP_TILES)
+                for product, table_t in ((by_cos, cos_t), (by_sin, sin_t)):
+                    nc.vector.scalar_tensor_tensor(
+                        out=product[:],
+                        in0=acc[:],
+                        scalar=bias_cols[:, tile_index : tile_index + 1],
+                        in1=table_t[:, c, :],
+                        op0=ADD,
+                        op1=MULT,
                     )
-                    y_halves = y[:].rearrange("p (h two i) -> p h two i", two=2, i=HALF)
-                    sin_halves = by_sin[:, jj, :].rearrange("p (h two i) -> p h two i", two=2, i=HALF)
-                    for two in range(2):
-                        nc.vector.tensor_tensor(
-                            out=sin_halves[:, :, two, :],
-                            in0=y_halves[:, :, 1 - two, :],
-                            in1=sin_split[:, b, two, :]
-                            .unsqueeze(1)
-                            .to_broadcast([P, GROUP_HEADS, HALF]),
-                            op=MULT,
-                        )
+                products.append((by_cos, by_sin))
+            return products
+
+        def finish_rotated(n, c, products):
+            for first in range(0, CHUNK_BLOCKS, PAIR):
                 rotated = work.tile([P, PAIR, GROUP], F32, tag="result")
-                nc.gpsimd.tensor_tensor(
-                    out=rotated[:].rearrange("p j (h i two) -> p (j h) i two", i=HALF, two=2),
-                    in0=by_cos[:].rearrange("p j (h two i) -> p (j h) i two", i=HALF, two=2),
-                    in1=by_sin[:].rearrange("p j (h two i) -> p (j h) i two", i=HALF, two=2),
-                    op=ADD,
-                )
+                for jj in range(PAIR):
+                    block = slice((first + jj) * P, (first + jj + 1) * P)
+                    total = psum_plain.tile([P, GROUP], F32, tag="plain")
+                    for m in range(GROUP_TILES):
+                        by_cos, by_sin = products[m]
+                        nc.tensor.matmul(
+                            out=total[:, m * P : (m + 1) * P],
+                            lhsT=by_cos[:, block],
+                            rhs=ident[:],
+                            is_transpose=True,
+                            start=True,
+                            stop=False,
+                        )
+                        nc.tensor.matmul(
+                            out=total[:, m * P : (m + 1) * P],
+                            lhsT=by_sin[:, block],
+                            rhs=swap[:],
+                            is_transpose=True,
+                            start=False,
+                            stop=True,
+                        )
+                    nc.scalar.copy(out=rotated[:, jj, :], in_=total[:])
                 store(n, c * CHUNK_BLOCKS + first, rotated)
 
         def project_plain(n, c):
             for first in range(0, CHUNK_BLOCKS, PAIR):
                 plain = work.tile([P, PAIR, GROUP], F32, tag="result")
                 for jj in range(PAIR):
-                    j = first + jj
+                    block = slice((first + jj) * P, (first + jj + 1) * P)
                     acc = psum_mx.tile([P, GROUP], F32, tag="acc")
                     for g in range(PASSES):
                         nc.tensor.matmul_mx(
                             out=acc[:],
-                            lhsT=x_codes[c][:, g, j * P : (j + 1) * P].bitcast(FP8X4),
-                            lhsT_scale=x_scales[c][:, g, j * P : (j + 1) * P],
+                            lhsT=x_codes[c][:, g, block].bitcast(FP8X4),
+                            lhsT_scale=x_scales[c][:, g, block],
                             rhs=w_codes[n][:, g, :].bitcast(FP8X4),
                             rhs_scale=w_scales[n][:, g, :],
                             start=(g == 0),
@@ -286,12 +282,41 @@ def tile_arlowvisionattention_pa_kernel(
                 in_=result[:],
             )
 
-        assert PASSES == CHUNKS
-        for n in range(GROUPS):
+        def quantise_ahead(unit):
+            assert PASSES == CHUNKS
+            step = unit + PASSES
+            if step < GROUPS * PASSES:
+                quantise_weights(step // PASSES, step % PASSES)
+
+        for g in range(PASSES):
+            quantise_weights(0, g)
+        quantise_positions(0)
+        waiting = None
+        for n in range(ROTATED_GROUPS):
             for c in range(CHUNKS):
-                if n + 1 < GROUPS:
-                    quantise_weights(n + 1, c)
-                if n < ROTATED_GROUPS:
-                    project_rotated(n, c)
-                else:
-                    project_plain(n, c)
+                if n == 0 and c > 0:
+                    quantise_positions(c)
+                quantise_ahead(n * CHUNKS + c)
+                products = multiply_rotated(n, c)
+                if waiting is not None:
+                    finish_rotated(*waiting)
+                waiting = (n, c, products)
+        finish_rotated(*waiting)
+
+        ones = const.tile([P, P], BF16)
+        nc.vector.memset(ones[:], 1.0)
+        v_bias = const.tile([P, WIDTH], F32)
+        for n in range(WIDTH // GROUP):
+            spread = psum_plain.tile([P, GROUP], F32, tag="plain")
+            nc.tensor.matmul(
+                out=spread[:],
+                lhsT=ones[:],
+                rhs=v_bias_row[:, n * GROUP : (n + 1) * GROUP],
+                start=True,
+                stop=True,
+            )
+            nc.scalar.copy(out=v_bias[:, n * GROUP : (n + 1) * GROUP], in_=spread[:])
+        for n in range(ROTATED_GROUPS, GROUPS):
+            for c in range(CHUNKS):
+                quantise_ahead(n * CHUNKS + c)
+                project_plain(n, c)

@@ -40,8 +40,9 @@ def tile_arlowvisionattention_pa_kernel(
         const = ctx.enter_context(tc.tile_pool(name="const", bufs=1))
         operands = ctx.enter_context(tc.tile_pool(name="operands", bufs=1))
         work = ctx.enter_context(tc.tile_pool(name="work", bufs=3))
-        psum_mx = ctx.enter_context(tc.psum_pool(name="psum_mx", bufs=5))
-        psum_plain = ctx.enter_context(tc.psum_pool(name="psum_plain", bufs=3))
+        psum_mx = ctx.enter_context(tc.psum_pool(name="psum_mx", bufs=4))
+        psum_plain = ctx.enter_context(tc.psum_pool(name="psum_plain", bufs=4))
+        ctx.enter_context(tc.manual_schedule())
 
         x_rows = hidden_states.rearrange("(p b) k -> p b k", b=S_BLOCKS)
         out_rows = [
@@ -128,6 +129,20 @@ def tile_arlowvisionattention_pa_kernel(
         bias_cols = const.tile([P, rotated_tiles], F32)
         nc.vector.tensor_copy(out=bias_cols[:], in_=bias_flipped[:, 0:rotated_tiles])
 
+        ones = const.tile([P, P], BF16)
+        nc.vector.memset(ones[:], 1.0)
+        v_bias = const.tile([P, WIDTH], F32)
+        for n in range(WIDTH // GROUP):
+            spread = psum_plain.tile([P, GROUP], F32, tag="plain")
+            nc.tensor.matmul(
+                out=spread[:],
+                lhsT=ones[:],
+                rhs=v_bias_row[:, n * GROUP : (n + 1) * GROUP],
+                start=True,
+                stop=True,
+            )
+            nc.scalar.copy(out=v_bias[:, n * GROUP : (n + 1) * GROUP], in_=spread[:])
+
         own_factor = const.tile([P, S_BLOCKS, TILE_HEADS, DH], F32)
         nc.vector.tensor_copy(
             out=own_factor[:],
@@ -158,12 +173,6 @@ def tile_arlowvisionattention_pa_kernel(
 
         cos_t = const.tile([P, CHUNKS, CHUNK], F32)
         sin_t = const.tile([P, CHUNKS, CHUNK], F32)
-        for c in range(CHUNKS):
-            for table, table_t in ((own_factor, cos_t), (neighbour_factor, sin_t)):
-                nc.scalar.copy(
-                    out=table_t[:, c, :],
-                    in_=flip_table(table, c)[:].rearrange("r j p -> r (j p)"),
-                )
 
         def quantise_weights(n, g):
             grouped = work.tile([P, GROUP, PACK], BF16, align_bytes=64, tag="w_grouped")
@@ -291,11 +300,16 @@ def tile_arlowvisionattention_pa_kernel(
         for g in range(PASSES):
             quantise_weights(0, g)
         quantise_positions(0)
+        for c in range(CHUNKS):
+            for table, table_t in ((own_factor, cos_t), (neighbour_factor, sin_t)):
+                nc.scalar.copy(
+                    out=table_t[:, c, :],
+                    in_=flip_table(table, c)[:].rearrange("r j p -> r (j p)"),
+                )
+        quantise_positions(1)
         waiting = None
         for n in range(ROTATED_GROUPS):
             for c in range(CHUNKS):
-                if n == 0 and c > 0:
-                    quantise_positions(c)
                 quantise_ahead(n * CHUNKS + c)
                 products = multiply_rotated(n, c)
                 if waiting is not None:
@@ -303,19 +317,6 @@ def tile_arlowvisionattention_pa_kernel(
                 waiting = (n, c, products)
         finish_rotated(*waiting)
 
-        ones = const.tile([P, P], BF16)
-        nc.vector.memset(ones[:], 1.0)
-        v_bias = const.tile([P, WIDTH], F32)
-        for n in range(WIDTH // GROUP):
-            spread = psum_plain.tile([P, GROUP], F32, tag="plain")
-            nc.tensor.matmul(
-                out=spread[:],
-                lhsT=ones[:],
-                rhs=v_bias_row[:, n * GROUP : (n + 1) * GROUP],
-                start=True,
-                stop=True,
-            )
-            nc.scalar.copy(out=v_bias[:, n * GROUP : (n + 1) * GROUP], in_=spread[:])
         for n in range(ROTATED_GROUPS, GROUPS):
             for c in range(CHUNKS):
                 quantise_ahead(n * CHUNKS + c)

@@ -10,6 +10,7 @@ U8 = mybir.dt.uint8
 FP8X4 = mybir.dt.float8_e4m3fn_x4
 ADD = mybir.AluOpType.add
 MULT = mybir.AluOpType.mult
+IDENTITY = mybir.ActivationFunctionType.Identity
 
 S, E, HEADS, DH = 1024, 1024, 16, 64
 WIDTH = HEADS * DH
@@ -28,6 +29,7 @@ ROTATED_GROUPS = 2 * WIDTH // GROUP
 GROUP_TILES = GROUP // P
 TILE_HEADS = P // DH
 PAIR = 2
+VECTOR_TILES = 3
 
 FLOPS = 2 * S * E * 3 * WIDTH
 
@@ -40,9 +42,8 @@ def tile_arlowvisionattention_pa_kernel(
         const = ctx.enter_context(tc.tile_pool(name="const", bufs=1))
         operands = ctx.enter_context(tc.tile_pool(name="operands", bufs=1))
         work = ctx.enter_context(tc.tile_pool(name="work", bufs=3))
-        psum_mx = ctx.enter_context(tc.psum_pool(name="psum_mx", bufs=4))
-        psum_plain = ctx.enter_context(tc.psum_pool(name="psum_plain", bufs=4))
-        ctx.enter_context(tc.manual_schedule())
+        psum_mx = ctx.enter_context(tc.psum_pool(name="psum_mx", bufs=5))
+        psum_plain = ctx.enter_context(tc.psum_pool(name="psum_plain", bufs=3))
 
         x_rows = hidden_states.rearrange("(p b) k -> p b k", b=S_BLOCKS)
         out_rows = [
@@ -129,20 +130,6 @@ def tile_arlowvisionattention_pa_kernel(
         bias_cols = const.tile([P, rotated_tiles], F32)
         nc.vector.tensor_copy(out=bias_cols[:], in_=bias_flipped[:, 0:rotated_tiles])
 
-        ones = const.tile([P, P], BF16)
-        nc.vector.memset(ones[:], 1.0)
-        v_bias = const.tile([P, WIDTH], F32)
-        for n in range(WIDTH // GROUP):
-            spread = psum_plain.tile([P, GROUP], F32, tag="plain")
-            nc.tensor.matmul(
-                out=spread[:],
-                lhsT=ones[:],
-                rhs=v_bias_row[:, n * GROUP : (n + 1) * GROUP],
-                start=True,
-                stop=True,
-            )
-            nc.scalar.copy(out=v_bias[:, n * GROUP : (n + 1) * GROUP], in_=spread[:])
-
         own_factor = const.tile([P, S_BLOCKS, TILE_HEADS, DH], F32)
         nc.vector.tensor_copy(
             out=own_factor[:],
@@ -173,6 +160,12 @@ def tile_arlowvisionattention_pa_kernel(
 
         cos_t = const.tile([P, CHUNKS, CHUNK], F32)
         sin_t = const.tile([P, CHUNKS, CHUNK], F32)
+        for c in range(CHUNKS):
+            for table, table_t in ((own_factor, cos_t), (neighbour_factor, sin_t)):
+                nc.scalar.copy(
+                    out=table_t[:, c, :],
+                    in_=flip_table(table, c)[:].rearrange("r j p -> r (j p)"),
+                )
 
         def quantise_weights(n, g):
             grouped = work.tile([P, GROUP, PACK], BF16, align_bytes=64, tag="w_grouped")
@@ -186,7 +179,7 @@ def tile_arlowvisionattention_pa_kernel(
                 in_=grouped[:].rearrange("q c t -> q (c t)"),
             )
 
-        def quantise_positions(c):
+        def quantise_positions(c, copy_out):
             grouped_words = x_grouped[c][:].bitcast(F32)
             for j in range(CHUNK_BLOCKS):
                 words = x_raw[c][:, j, :].bitcast(F32)
@@ -195,7 +188,7 @@ def tile_arlowvisionattention_pa_kernel(
                     nc.tensor.transpose(
                         out=flipped[:, gu, :], in_=words[:, gu * P : (gu + 1) * P], identity=ident[:]
                     )
-                nc.vector.tensor_copy(
+                copy_out(
                     out=grouped_words[:, :, j * P : (j + 1) * P, :],
                     in_=flipped[:].rearrange("q (g u) s -> q g s u", u=2),
                 )
@@ -223,15 +216,26 @@ def tile_arlowvisionattention_pa_kernel(
                 tile_index = n * GROUP_TILES + m
                 by_cos = work.tile([P, CHUNK], F32, tag="by_cos", bufs=2 * GROUP_TILES)
                 by_sin = work.tile([P, CHUNK], F32, tag="by_sin", bufs=2 * GROUP_TILES)
-                for product, table_t in ((by_cos, cos_t), (by_sin, sin_t)):
-                    nc.vector.scalar_tensor_tensor(
-                        out=product[:],
-                        in0=acc[:],
-                        scalar=bias_cols[:, tile_index : tile_index + 1],
-                        in1=table_t[:, c, :],
-                        op0=ADD,
-                        op1=MULT,
+                bias = bias_cols[:, tile_index : tile_index + 1]
+                if m < VECTOR_TILES:
+                    for product, table_t in ((by_cos, cos_t), (by_sin, sin_t)):
+                        nc.vector.scalar_tensor_tensor(
+                            out=product[:],
+                            in0=acc[:],
+                            scalar=bias,
+                            in1=table_t[:, c, :],
+                            op0=ADD,
+                            op1=MULT,
+                        )
+                else:
+                    with_bias = work.tile([P, CHUNK], F32, tag="with_bias")
+                    nc.scalar.activation(
+                        out=with_bias[:], in_=acc[:], func=IDENTITY, bias=bias, scale=1.0
                     )
+                    for product, table_t in ((by_cos, cos_t), (by_sin, sin_t)):
+                        nc.gpsimd.tensor_tensor(
+                            out=product[:], in0=with_bias[:], in1=table_t[:, c, :], op=MULT
+                        )
                 products.append((by_cos, by_sin))
             return products
 
@@ -299,17 +303,12 @@ def tile_arlowvisionattention_pa_kernel(
 
         for g in range(PASSES):
             quantise_weights(0, g)
-        quantise_positions(0)
-        for c in range(CHUNKS):
-            for table, table_t in ((own_factor, cos_t), (neighbour_factor, sin_t)):
-                nc.scalar.copy(
-                    out=table_t[:, c, :],
-                    in_=flip_table(table, c)[:].rearrange("r j p -> r (j p)"),
-                )
-        quantise_positions(1)
+        quantise_positions(0, nc.vector.tensor_copy)
         waiting = None
         for n in range(ROTATED_GROUPS):
             for c in range(CHUNKS):
+                if n == 0 and c > 0:
+                    quantise_positions(c, nc.scalar.copy)
                 quantise_ahead(n * CHUNKS + c)
                 products = multiply_rotated(n, c)
                 if waiting is not None:
@@ -317,6 +316,19 @@ def tile_arlowvisionattention_pa_kernel(
                 waiting = (n, c, products)
         finish_rotated(*waiting)
 
+        ones = const.tile([P, P], BF16)
+        nc.vector.memset(ones[:], 1.0)
+        v_bias = const.tile([P, WIDTH], F32)
+        for n in range(WIDTH // GROUP):
+            spread = psum_plain.tile([P, GROUP], F32, tag="plain")
+            nc.tensor.matmul(
+                out=spread[:],
+                lhsT=ones[:],
+                rhs=v_bias_row[:, n * GROUP : (n + 1) * GROUP],
+                start=True,
+                stop=True,
+            )
+            nc.scalar.copy(out=v_bias[:, n * GROUP : (n + 1) * GROUP], in_=spread[:])
         for n in range(ROTATED_GROUPS, GROUPS):
             for c in range(CHUNKS):
                 quantise_ahead(n * CHUNKS + c)

from contextlib import ExitStack

import concourse.mybir as mybir
from concourse.masks import make_identity

F32 = mybir.dt.float32
BF16 = mybir.dt.bfloat16
U32 = mybir.dt.uint32
U8 = mybir.dt.uint8
FP8X4 = mybir.dt.float8_e4m3fn_x4
ADD = mybir.AluOpType.add
MULT = mybir.AluOpType.mult
IDENTITY = mybir.ActivationFunctionType.Identity

S, E, HEADS, DH = 1024, 1024, 16, 64
WIDTH = HEADS * DH
HALF = DH // 2
P = 128
PACK = 4
K_PASS = P * PACK
PASSES = E // K_PASS
S_BLOCKS = S // P
CHUNK_BLOCKS = 4
CHUNK = CHUNK_BLOCKS * P
CHUNKS = S_BLOCKS // CHUNK_BLOCKS
GROUP = 512
GROUPS = 3 * WIDTH // GROUP
ROTATED_GROUPS = 2 * WIDTH // GROUP
GROUP_TILES = GROUP // P
TILE_HEADS = P // DH
PAIR = 2
VECTOR_TILES = 3

FLOPS = 2 * S * E * 3 * WIDTH


def tile_arlowvisionattention_pa_kernel(
    tc, hidden_states, cos, sin, w_qkv, b_qkv, out_0, out_1, out_2
):
    nc = tc.nc
    with ExitStack() as ctx:
        const = ctx.enter_context(tc.tile_pool(name="const", bufs=1))
        operands = ctx.enter_context(tc.tile_pool(name="operands", bufs=1))
        work = ctx.enter_context(tc.tile_pool(name="work", bufs=3))
        psum_mx = ctx.enter_context(tc.psum_pool(name="psum_mx", bufs=5))
        psum_plain = ctx.enter_context(tc.psum_pool(name="psum_plain", bufs=3))

        x_rows = hidden_states.rearrange("(p b) k -> p b k", b=S_BLOCKS)
        out_rows = [
            out.rearrange("(p b) h d -> p b (h d)", b=S_BLOCKS) for out in (out_0, out_1, out_2)
        ]

        x_raw = [
            operands.tile([P, CHUNK_BLOCKS, E], BF16, name="x_raw%d" % c) for c in range(CHUNKS)
        ]
        x_grouped = [
            operands.tile([P, PASSES, CHUNK, PACK], BF16, name="x_grouped%d" % c, align_bytes=64)
            for c in range(CHUNKS)
        ]
        x_codes = [
            operands.tile([P, PASSES, CHUNK], U32, name="x_codes%d" % c, align_bytes=64)
            for c in range(CHUNKS)
        ]
        x_scales = [
            operands.tile([P, PASSES, CHUNK], U8, name="x_scales%d" % c, align_bytes=64)
            for c in range(CHUNKS)
        ]
        w_raw = [
            operands.tile([P, PASSES, PACK, GROUP], BF16, name="w_raw%d" % n) for n in range(GROUPS)
        ]
        w_codes = [
            operands.tile([P, PASSES, GROUP], U32, name="w_codes%d" % n, align_bytes=64)
            for n in range(GROUPS)
        ]
        w_scales = [
            operands.tile([P, PASSES, GROUP], U8, name="w_scales%d" % n, align_bytes=64)
            for n in range(GROUPS)
        ]

        cos_raw = const.tile([P, S_BLOCKS, DH], BF16)
        sin_raw = const.tile([P, S_BLOCKS, DH], BF16)
        nc.scalar.dma_start(out=cos_raw[:], in_=cos.rearrange("(p b) d -> p b d", b=S_BLOCKS))
        nc.scalar.dma_start(out=sin_raw[:], in_=sin.rearrange("(p b) d -> p b d", b=S_BLOCKS))

        rotated_tiles = ROTATED_GROUPS * GROUP_TILES
        bias_rows = const.tile([P, P], BF16)
        nc.vector.memset(bias_rows[:], 0.0)
        nc.scalar.dma_start(
            out=bias_rows[0:rotated_tiles, :],
            in_=b_qkv[0 : rotated_tiles * P].rearrange("(t n) -> t n", n=P),
        )
        v_bias_row = const.tile([P, WIDTH], BF16)
        nc.vector.memset(v_bias_row[:], 0.0)
        nc.scalar.dma_start(
            out=v_bias_row[0:1, :],
            in_=b_qkv[2 * WIDTH : 3 * WIDTH].rearrange("(o n) -> o n", o=1),
        )

        def load_weights(n):
            for g in range(PASSES):
                for u in range(PACK // 2):
                    first = g * K_PASS + u * 2 * P
                    nc.sync.dma_start(
                        out=w_raw[n][:, g, 2 * u : 2 * u + 2, :],
                        in_=w_qkv[first : first + 2 * P, n * GROUP : (n + 1) * GROUP].rearrange(
                            "(q e) n -> q e n", e=2
                        ),
                    )

        load_weights(0)
        for c in range(CHUNKS):
            nc.sync.dma_start(
                out=x_raw[c][:], in_=x_rows[:, c * CHUNK_BLOCKS : (c + 1) * CHUNK_BLOCKS, :]
            )
        for n in range(1, GROUPS):
            load_weights(n)

        ident = const.tile([P, P], F32)
        make_identity(nc, ident[:])
        swap = const.tile([P, P], F32)
        swap_pairs = swap[:].rearrange("r (i two) -> r i two", two=2)
        ident_pairs = ident[:].rearrange("r (i two) -> r i two", two=2)
        for two in range(2):
            nc.vector.tensor_copy(out=swap_pairs[:, :, two], in_=ident_pairs[:, :, 1 - two])

        bias_rows_f32 = const.tile([P, P], F32)
        nc.vector.tensor_copy(out=bias_rows_f32[:], in_=bias_rows[:])
        bias_flipped = psum_plain.tile([P, P], F32, tag="plain")
        nc.tensor.transpose(out=bias_flipped[:], in_=bias_rows_f32[:], identity=ident[:])
        bias_cols = const.tile([P, rotated_tiles], F32)
        nc.vector.tensor_copy(out=bias_cols[:], in_=bias_flipped[:, 0:rotated_tiles])

        own_factor = const.tile([P, S_BLOCKS, TILE_HEADS, DH], F32)
        nc.vector.tensor_copy(
            out=own_factor[:],
            in_=cos_raw[:].unsqueeze(2).to_broadcast([P, S_BLOCKS, TILE_HEADS, DH]),
        )
        sin_pairs = sin_raw[:].rearrange("p b (i two) -> p b i two", two=2)
        crossed = const.tile([P, S_BLOCKS, HALF, 2], F32)
        nc.vector.tensor_copy(out=crossed[:, :, :, 0], in_=sin_pairs[:, :, :, 1])
        nc.vector.tensor_scalar_mul(out=crossed[:, :, :, 1], in0=sin_pairs[:, :, :, 0], scalar1=-1.0)
        neighbour_factor = const.tile([P, S_BLOCKS, TILE_HEADS, DH], F32)
        nc.vector.tensor_copy(
            out=neighbour_factor[:],
            in_=crossed[:]
            .rearrange("p b i two -> p b (i two)")
            .unsqueeze(2)
            .to_broadcast([P, S_BLOCKS, TILE_HEADS, DH]),
        )

        def flip_table(table, c):
            flipped = psum_plain.tile([P, CHUNK_BLOCKS, P], F32, tag="plain")
            for j in range(CHUNK_BLOCKS):
                nc.tensor.transpose(
                    out=flipped[:, j, :],
                    in_=table[:, c * CHUNK_BLOCKS + j, :, :].rearrange("p h d -> p (h d)"),
                    identity=ident[:],
                )
            return flipped

        cos_t = const.tile([P, CHUNKS, CHUNK], F32)
        sin_t = const.tile([P, CHUNKS, CHUNK], F32)
        for c in range(CHUNKS):
            for table, table_t in ((own_factor, cos_t), (neighbour_factor, sin_t)):
                nc.scalar.copy(
                    out=table_t[:, c, :],
                    in_=flip_table(table, c)[:].rearrange("r j p -> r (j p)"),
                )

        def quantise_weights(n, g):
            grouped = work.tile([P, GROUP, PACK], BF16, align_bytes=64, tag="w_grouped")
            nc.scalar.copy(
                out=grouped[:].rearrange("q (c i) t -> q c t i", i=4),
                in_=w_raw[n][:, g, :, :].rearrange("q t (c i) -> q c t i", i=4),
            )
            nc.vector.quantize_mx(
                out=w_codes[n][:, g, :].bitcast(FP8X4),
                scales=w_scales[n][:, g, :],
                in_=grouped[:].rearrange("q c t -> q (c t)"),
            )

        def quantise_positions(c, copy_out):
            grouped_words = x_grouped[c][:].bitcast(F32)
            for j in range(CHUNK_BLOCKS):
                words = x_raw[c][:, j, :].bitcast(F32)
                flipped = psum_plain.tile([P, PASSES * 2, P], F32, tag="plain")
                for gu in range(PASSES * 2):
                    nc.tensor.transpose(
                        out=flipped[:, gu, :], in_=words[:, gu * P : (gu + 1) * P], identity=ident[:]
                    )
                copy_out(
                    out=grouped_words[:, :, j * P : (j + 1) * P, :],
                    in_=flipped[:].rearrange("q (g u) s -> q g s u", u=2),
                )
            for g in range(PASSES):
                nc.vector.quantize_mx(
                    out=x_codes[c][:, g, :].bitcast(FP8X4),
                    scales=x_scales[c][:, g, :],
                    in_=x_grouped[c][:, g, :, :].rearrange("q s t -> q (s t)"),
                )

        def multiply_rotated(n, c):
            products = []
            for m in range(GROUP_TILES):
                acc = psum_mx.tile([P, CHUNK], F32, tag="acc")
                for g in range(PASSES):
                    nc.tensor.matmul_mx(
                        out=acc[:],
                        lhsT=w_codes[n][:, g, m * P : (m + 1) * P].bitcast(FP8X4),
                        lhsT_scale=w_scales[n][:, g, m * P : (m + 1) * P],
                        rhs=x_codes[c][:, g, :].bitcast(FP8X4),
                        rhs_scale=x_scales[c][:, g, :],
                        start=(g == 0),
                        stop=(g == PASSES - 1),
                    )
                tile_index = n * GROUP_TILES + m
                by_cos = work.tile([P, CHUNK], F32, tag="by_cos", bufs=2 * GROUP_TILES)
                by_sin = work.tile([P, CHUNK], F32, tag="by_sin", bufs=2 * GROUP_TILES)
                bias = bias_cols[:, tile_index : tile_index + 1]
                if m < VECTOR_TILES:
                    for product, table_t in ((by_cos, cos_t), (by_sin, sin_t)):
                        nc.vector.scalar_tensor_tensor(
                            out=product[:],
                            in0=acc[:],
                            scalar=bias,
                            in1=table_t[:, c, :],
                            op0=ADD,
                            op1=MULT,
                        )
                else:
                    with_bias = work.tile([P, CHUNK], F32, tag="with_bias")
                    nc.scalar.activation(
                        out=with_bias[:], in_=acc[:], func=IDENTITY, bias=bias, scale=1.0
                    )
                    for product, table_t in ((by_cos, cos_t), (by_sin, sin_t)):
                        nc.gpsimd.tensor_tensor(
                            out=product[:], in0=with_bias[:], in1=table_t[:, c, :], op=MULT
                        )
                products.append((by_cos, by_sin))
            return products

        def finish_rotated(n, c, products):
            for first in range(0, CHUNK_BLOCKS, PAIR):
                rotated = work.tile([P, PAIR, GROUP], F32, tag="result")
                for jj in range(PAIR):
                    block = slice((first + jj) * P, (first + jj + 1) * P)
                    total = psum_plain.tile([P, GROUP], F32, tag="plain")
                    for m in range(GROUP_TILES):
                        by_cos, by_sin = products[m]
                        nc.tensor.matmul(
                            out=total[:, m * P : (m + 1) * P],
                            lhsT=by_cos[:, block],
                            rhs=ident[:],
                            is_transpose=True,
                            start=True,
                            stop=False,
                        )
                        nc.tensor.matmul(
                            out=total[:, m * P : (m + 1) * P],
                            lhsT=by_sin[:, block],
                            rhs=swap[:],
                            is_transpose=True,
                            start=False,
                            stop=True,
                        )
                    nc.scalar.copy(out=rotated[:, jj, :], in_=total[:])
                store(n, c * CHUNK_BLOCKS + first, rotated)

        def project_plain(n, c):
            for first in range(0, CHUNK_BLOCKS, PAIR):
                plain = work.tile([P, PAIR, GROUP], F32, tag="result")
                for jj in range(PAIR):
                    block = slice((first + jj) * P, (first + jj + 1) * P)
                    acc = psum_mx.tile([P, GROUP], F32, tag="acc")
                    for g in range(PASSES):
                        nc.tensor.matmul_mx(
                            out=acc[:],
                            lhsT=x_codes[c][:, g, block].bitcast(FP8X4),
                            lhsT_scale=x_scales[c][:, g, block],
                            rhs=w_codes[n][:, g, :].bitcast(FP8X4),
                            rhs_scale=w_scales[n][:, g, :],
                            start=(g == 0),
                            stop=(g == PASSES - 1),
                        )
                    col = (n - ROTATED_GROUPS) * GROUP
                    nc.vector.tensor_tensor(
                        out=plain[:, jj, :], in0=acc[:], in1=v_bias[:, col : col + GROUP], op=ADD
                    )
                store(n, c * CHUNK_BLOCKS + first, plain)

        def store(n, first_block, result):
            which, col = divmod(n * GROUP, WIDTH)
            nc.sync.dma_start(
                out=out_rows[which][:, first_block : first_block + PAIR, col : col + GROUP],
                in_=result[:],
            )

        def quantise_ahead(unit):
            assert PASSES == CHUNKS
            step = unit + PASSES
            if step < GROUPS * PASSES:
                quantise_weights(step // PASSES, step % PASSES)

        for g in range(PASSES):
            quantise_weights(0, g)
        quantise_positions(0, nc.vector.tensor_copy)
        waiting = None
        for n in range(ROTATED_GROUPS):
            for c in range(CHUNKS):
                if n == 0 and c > 0:
                    quantise_positions(c, nc.scalar.copy)
                quantise_ahead(n * CHUNKS + c)
                products = multiply_rotated(n, c)
                if waiting is not None:
                    finish_rotated(*waiting)
                waiting = (n, c, products)
        finish_rotated(*waiting)

        ones = const.tile([P, P], BF16)
        nc.vector.memset(ones[:], 1.0)
        v_bias = const.tile([P, WIDTH], F32)
        for n in range(WIDTH // GROUP):
            spread = psum_plain.tile([P, GROUP], F32, tag="plain")
            nc.tensor.matmul(
                out=spread[:],
                lhsT=ones[:],
                rhs=v_bias_row[:, n * GROUP : (n + 1) * GROUP],
                start=True,
                stop=True,
            )
            nc.scalar.copy(out=v_bias[:, n * GROUP : (n + 1) * GROUP], in_=spread[:])
        for n in range(ROTATED_GROUPS, GROUPS):
            for c in range(CHUNKS):
                quantise_ahead(n * CHUNKS + c)
                project_plain(n, c)
